import numpy as np
import ml_dtypes


def mxq(x, axis, fmt="e4m3"):
    dtype, down = {"e4m3": (ml_dtypes.float8_e4m3fn, 7), "e5m2": (ml_dtypes.float8_e5m2, 14)}[fmt]
    v = np.moveaxis(np.asarray(x, np.float32).astype(ml_dtypes.bfloat16).astype(np.float64), axis, -1)
    blocks = v.reshape(v.shape[:-1] + (-1, 32))
    amax = np.abs(blocks).max(-1, keepdims=True)
    byte = np.maximum(np.where(amax > 0, np.frexp(amax)[1] - 1 + 127, 0) - down, 1)
    scale = np.exp2(byte - 127.0)
    codes = (blocks / scale).astype(np.float32).astype(dtype).astype(np.float64)
    return np.moveaxis((codes * scale).reshape(v.shape), -1, axis)


WIDE = False


def mx_kscale(k):
    if not WIDE:
        return np.ones(k)
    levels = np.array([20, -20, 10, -10, 0])
    a = np.random.permutation(np.resize(levels, k // 512 * 4)).reshape(k // 512, 4)
    idx = np.arange(k)
    return np.exp2(a[idx // 512, idx % 128 // 32])


BF16 = ml_dtypes.bfloat16


def bf(x):
    return np.asarray(x, np.float32).astype(BF16)


def f64(x):
    return np.asarray(x).astype(np.float64)


N, C, O, TH, TW = 2, 1024, 512, 32, 32
BN_EPS = 1e-5
IMG_SIZES = [(max(TH >> (l + 1), 1), max(TW >> (l + 1), 1)) for l in range(5)]


def setup_inputs():
    u = mx_kscale(O)
    inp = {}
    for l, (h, w) in enumerate(IMG_SIZES):
        inp[f'img_feat{l}'] = bf(np.random.standard_normal((N, C, h, w)) * 0.5)
    inp['pts_feat0'] = bf(np.random.standard_normal((N, C, TH, TW)))
    inp['img_w'] = bf(np.random.standard_normal((O, C)) / np.sqrt(C))
    inp['img_b'] = bf(np.random.standard_normal(O) * 0.1)
    inp['img_gamma'] = bf(1.0 + 0.1 * np.random.standard_normal(O))
    inp['img_beta'] = bf(np.random.standard_normal(O) * 0.1)
    inp['img_mean'] = bf(np.random.standard_normal(O) * 0.1)
    inp['img_var'] = bf(np.random.uniform(0.5, 1.5, O))
    w0 = bf(np.random.standard_normal((O, C)) / np.sqrt(C))
    inp['pts_w'] = bf(f64(w0) / u[:, None])
    inp['pts_b'] = bf(np.random.standard_normal(O) * 0.1)
    inp['pts_gamma'] = bf(1.0 + 0.1 * np.random.standard_normal(O))
    inp['pts_beta'] = bf(np.random.standard_normal(O) * 0.1)
    inp['pts_mean'] = bf(np.random.standard_normal(O) * 0.1)
    inp['pts_var'] = bf(np.random.uniform(0.5, 1.5, O))
    y = (f64(w0) @ f64(inp['pts_feat0']).reshape(N, C, TH * TW)).reshape(N, O, TH, TW) + f64(inp['pts_b'])[None, :, None, None]
    scale = f64(inp['pts_gamma']) / np.sqrt(f64(inp['pts_var']) + BN_EPS)
    z = (y - f64(inp['pts_mean'])[None, :, None, None]) * scale[None, :, None, None] + f64(inp['pts_beta'])[None, :, None, None]
    inp['pts_z'] = np.asarray(z, np.float32)
    g = np.random.standard_normal((N, 2 * O, TH, TW)) * np.exp2(np.random.randint(-12, 1, (N, 1, TH, TW))) * 32.0
    g[:, O:] = g[:, O:] * u[None, :, None, None]
    inp['grad_out'] = bf(g)
    return inp


def reference(img_feat0, img_feat1, img_feat2, img_feat3, img_feat4, pts_feat0,
              img_w, img_b, img_gamma, img_beta, img_mean, img_var,
              pts_w, pts_b, pts_gamma, pts_beta, pts_mean, pts_var, pts_z, grad_out):
    g = f64(grad_out)[:, O:]
    scale = f64(pts_gamma) / np.sqrt(f64(pts_var) + BN_EPS)
    dy = g * (f64(pts_z) > 0.0) * scale[None, :, None, None]
    n, o, h, w = dy.shape
    dyq = mxq(dy, 1, 'e5m2').reshape(n, o, h * w)
    wq = mxq(f64(pts_w), 0, 'e4m3')
    return (wq.T @ dyq).reshape(n, -1, h, w)

@@ -1,0 +1,140 @@
+from contextlib import ExitStack
+
+import concourse.mybir as mybir
+
+BF16 = mybir.dt.bfloat16
+F32 = mybir.dt.float32
+U32 = mybir.dt.uint32
+U8 = mybir.dt.uint8
+E4M3_X4 = mybir.dt.float8_e4m3fn_x4
+E5M2_X4 = mybir.dt.float8_e5m2_x4
+ALU = mybir.AluOpType
+ACT = mybir.ActivationFunctionType
+
+P = 128
+PACK = 4
+IMAGES = 2
+OUT_CH = 512
+IN_CH = 1024
+PIXELS = 1024
+N_TILE = 512
+HALVES = PIXELS // N_TILE
+M_TILES = IN_CH // P
+STORE_TILES = 2
+BN_EPS = 1e-5
+
+FLOPS = 2 * IMAGES * PIXELS * IN_CH * OUT_CH
+BYTES = (
+    IMAGES * OUT_CH * PIXELS * (2 + 4)
+    + OUT_CH * IN_CH * 2
+    + 2 * OUT_CH * 2
+    + IMAGES * IN_CH * PIXELS * 4
+)
+
+
+def tile_prefusioncat_t_v_kernel(
+    tc,
+    img_feat0, img_feat1, img_feat2, img_feat3, img_feat4, pts_feat0,
+    img_w, img_b, img_gamma, img_beta, img_mean, img_var,
+    pts_w, pts_b, pts_gamma, pts_beta, pts_mean, pts_var, pts_z, grad_out,
+    out,
+):
+    nc = tc.nc
+    with ExitStack() as ctx:
+        keep = ctx.enter_context(tc.tile_pool(name="keep", bufs=1))
+        psum = ctx.enter_context(tc.psum_pool(name="psum", bufs=8))
+
+        gamma_bf = keep.tile([P, PACK], BF16)
+        var_bf = keep.tile([P, PACK], BF16)
+        nc.scalar.dma_start(out=var_bf[:], in_=pts_var.rearrange("(p j) -> p j", j=PACK))
+        nc.scalar.dma_start(out=gamma_bf[:], in_=pts_gamma.rearrange("(p j) -> p j", j=PACK))
+
+        w_raw = keep.tile([P, PACK, IN_CH], BF16)
+        nc.sync.dma_start(out=w_raw[:], in_=pts_w.rearrange("(p j) c -> p j c", j=PACK))
+        g_raw = []
+        z_raw = []
+        for n in range(IMAGES):
+            g_n = keep.tile([P, PACK, PIXELS], BF16, name="g_raw%d" % n)
+            z_n = keep.tile([P, PACK, PIXELS], F32, name="z_raw%d" % n)
+            nc.sync.dma_start(
+                out=g_n[:],
+                in_=grad_out[n, OUT_CH : 2 * OUT_CH].rearrange("(p j) h w -> p j (h w)", j=PACK),
+            )
+            nc.sync.dma_start(out=z_n[:], in_=pts_z[n].rearrange("(p j) h w -> p j (h w)", j=PACK))
+            g_raw.append(g_n)
+            z_raw.append(z_n)
+
+        var_eps = keep.tile([P, PACK], F32)
+        std = keep.tile([P, PACK], F32)
+        inv_std = keep.tile([P, PACK], F32)
+        scale = keep.tile([P, PACK], F32)
+        nc.vector.tensor_scalar_add(out=var_eps[:], in0=var_bf[:], scalar1=BN_EPS)
+        nc.scalar.sqrt(std[:], var_eps[:])
+        nc.vector.reciprocal(out=inv_std[:], in_=std[:])
+        nc.vector.tensor_mul(out=scale[:], in0=inv_std[:], in1=gamma_bf[:])
+
+        w_grouped = keep.tile([P, M_TILES, P, PACK], BF16, align_bytes=64)
+        w_codes = keep.tile([P, M_TILES * P], U32, align_bytes=64)
+        w_scales = keep.tile([P, M_TILES * P], U8, align_bytes=64)
+        w_by_tile = w_raw[:].rearrange("p j (m t) -> p t m j", t=M_TILES)
+        half_tiles = M_TILES // 2
+        for first in range(0, M_TILES, half_tiles):
+            nc.vector.tensor_copy(
+                out=w_grouped[:, first : first + half_tiles],
+                in_=w_by_tile[:, first : first + half_tiles],
+            )
+        for first in range(0, M_TILES, half_tiles):
+            cols = slice(first * P, (first + half_tiles) * P)
+            nc.vector.quantize_mx(
+                out=w_codes[:, cols].bitcast(E4M3_X4),
+                scales=w_scales[:, cols],
+                in_=w_grouped[:, first : first + half_tiles].rearrange("p t m j -> p (t m j)"),
+            )
+
+        out_by_tile = out.rearrange("n (m t) h w -> n m t (h w)", t=M_TILES)
+        banks_emptied = 0
+        for n in range(IMAGES):
+            g_scaled = keep.tile([P, PACK, PIXELS], BF16, name="g_scaled%d" % n)
+            for j in range(PACK):
+                nc.scalar.activation(
+                    out=g_scaled[:, j, :], in_=g_raw[n][:, j, :], func=ACT.Copy, scale=scale[:, j : j + 1]
+                )
+
+            out_sb = keep.tile([P, M_TILES, PIXELS], F32, name="out_sb%d" % n)
+            for h in range(HALVES):
+                px = slice(h * N_TILE, (h + 1) * N_TILE)
+                dy_grouped = keep.tile([P, N_TILE, PACK], BF16, align_bytes=64, name="dy_grouped%d%d" % (n, h))
+                dy_codes = keep.tile([P, N_TILE], U32, align_bytes=64, name="dy_codes%d%d" % (n, h))
+                dy_scales = keep.tile([P, N_TILE], U8, align_bytes=64, name="dy_scales%d%d" % (n, h))
+                nc.vector.scalar_tensor_tensor(
+                    out=dy_grouped[:],
+                    in0=z_raw[n][:, :, px].rearrange("p j x -> p x j"),
+                    scalar=0.0,
+                    in1=g_scaled[:, :, px].rearrange("p j x -> p x j"),
+                    op0=ALU.is_gt,
+                    op1=ALU.mult,
+                )
+                nc.vector.quantize_mx(
+                    out=dy_codes[:].bitcast(E5M2_X4),
+                    scales=dy_scales[:],
+                    in_=dy_grouped[:].rearrange("p x j -> p (x j)"),
+                )
+                for t in range(M_TILES):
+                    acc = psum.tile([P, N_TILE], F32)
+                    nc.tensor.matmul_mx(
+                        out=acc[:],
+                        lhsT=w_codes[:, t * P : (t + 1) * P].bitcast(E4M3_X4),
+                        lhsT_scale=w_scales[:, t * P : (t + 1) * P],
+                        rhs=dy_codes[:].bitcast(E5M2_X4),
+                        rhs_scale=dy_scales[:],
+                        start=True,
+                        stop=True,
+                    )
+                    if banks_emptied % 3 == 2:
+                        nc.vector.tensor_copy(out=out_sb[:, t, px], in_=acc[:])
+                    else:
+                        nc.scalar.copy(out=out_sb[:, t, px], in_=acc[:])
+                    banks_emptied += 1
+                    if h == HALVES - 1 and t % STORE_TILES == STORE_TILES - 1:
+                        tiles = slice(t + 1 - STORE_TILES, t + 1)
+                        nc.sync.dma_start(out=out_by_tile[n, :, tiles, :], in_=out_sb[:, tiles, :])

@@ -9,7 +9,6 @@ U8 = mybir.dt.uint8
 E4M3_X4 = mybir.dt.float8_e4m3fn_x4
 E5M2_X4 = mybir.dt.float8_e5m2_x4
 ALU = mybir.AluOpType
-ACT = mybir.ActivationFunctionType
 
 P = 128
 PACK = 4
@@ -19,8 +18,9 @@ IN_CH = 1024
 PIXELS = 1024
 N_TILE = 512
 HALVES = PIXELS // N_TILE
-M_TILES = IN_CH // P
-STORE_TILES = 2
+PAIR = 2
+PAIRS = IN_CH // (P * PAIR)
+PSUM_BANKS = 8
 BN_EPS = 1e-5
 
 FLOPS = 2 * IMAGES * PIXELS * IN_CH * OUT_CH
@@ -42,7 +42,7 @@ def tile_prefusioncat_t_v_kernel(
     nc = tc.nc
     with ExitStack() as ctx:
         keep = ctx.enter_context(tc.tile_pool(name="keep", bufs=1))
-        psum = ctx.enter_context(tc.psum_pool(name="psum", bufs=8))
+        psum = ctx.enter_context(tc.psum_pool(name="psum", bufs=PSUM_BANKS))
 
         gamma_bf = keep.tile([P, PACK], BF16)
         var_bf = keep.tile([P, PACK], BF16)
@@ -60,7 +60,10 @@ def tile_prefusioncat_t_v_kernel(
                 out=g_n[:],
                 in_=grad_out[n, OUT_CH : 2 * OUT_CH].rearrange("(p j) h w -> p j (h w)", j=PACK),
             )
-            nc.sync.dma_start(out=z_n[:], in_=pts_z[n].rearrange("(p j) h w -> p j (h w)", j=PACK))
+            z_dram = pts_z[n].rearrange("(p j) h w -> p j (h w)", j=PACK)
+            for h in range(HALVES):
+                px = slice(h * N_TILE, (h + 1) * N_TILE)
+                nc.sync.dma_start(out=z_n[:, :, px], in_=z_dram[:, :, px])
             g_raw.append(g_n)
             z_raw.append(z_n)
 
@@ -73,39 +76,32 @@ def tile_prefusioncat_t_v_kernel(
         nc.vector.reciprocal(out=inv_std[:], in_=std[:])
         nc.vector.tensor_mul(out=scale[:], in0=inv_std[:], in1=gamma_bf[:])
 
-        w_grouped = keep.tile([P, M_TILES, P, PACK], BF16, align_bytes=64)
-        w_codes = keep.tile([P, M_TILES * P], U32, align_bytes=64)
-        w_scales = keep.tile([P, M_TILES * P], U8, align_bytes=64)
-        w_by_tile = w_raw[:].rearrange("p j (m t) -> p t m j", t=M_TILES)
-        half_tiles = M_TILES // 2
-        for first in range(0, M_TILES, half_tiles):
-            nc.vector.tensor_copy(
-                out=w_grouped[:, first : first + half_tiles],
-                in_=w_by_tile[:, first : first + half_tiles],
-            )
-        for first in range(0, M_TILES, half_tiles):
-            cols = slice(first * P, (first + half_tiles) * P)
+        w_grouped = keep.tile([P, PAIRS, PAIR, P, PACK], BF16, align_bytes=64)
+        w_codes = keep.tile([P, PAIRS, PAIR, P], U32, align_bytes=64)
+        w_scales = keep.tile([P, PAIRS, PAIR, P], U8, align_bytes=64)
+        w_by_pair = w_raw[:].rearrange("p j (a m b) -> p a b m j", m=P, b=PAIR)
+        for a in range(PAIRS):
+            nc.vector.tensor_copy(out=w_grouped[:, a], in_=w_by_pair[:, a])
+        for a in range(0, PAIRS, 2):
             nc.vector.quantize_mx(
-                out=w_codes[:, cols].bitcast(E4M3_X4),
-                scales=w_scales[:, cols],
-                in_=w_grouped[:, first : first + half_tiles].rearrange("p t m j -> p (t m j)"),
+                out=w_codes[:, a : a + 2].rearrange("p a b m -> p (a b m)").bitcast(E4M3_X4),
+                scales=w_scales[:, a : a + 2].rearrange("p a b m -> p (a b m)"),
+                in_=w_grouped[:, a : a + 2].rearrange("p a b m j -> p (a b m j)"),
             )
 
-        out_by_tile = out.rearrange("n (m t) h w -> n m t (h w)", t=M_TILES)
-        banks_emptied = 0
+        dy_codes = []
+        dy_scales = []
         for n in range(IMAGES):
             g_scaled = keep.tile([P, PACK, PIXELS], BF16, name="g_scaled%d" % n)
             for j in range(PACK):
-                nc.scalar.activation(
-                    out=g_scaled[:, j, :], in_=g_raw[n][:, j, :], func=ACT.Copy, scale=scale[:, j : j + 1]
+                nc.vector.tensor_scalar_mul(
+                    out=g_scaled[:, j, :], in0=g_raw[n][:, j, :], scalar1=scale[:, j : j + 1]
                 )
-
-            out_sb = keep.tile([P, M_TILES, PIXELS], F32, name="out_sb%d" % n)
             for h in range(HALVES):
                 px = slice(h * N_TILE, (h + 1) * N_TILE)
                 dy_grouped = keep.tile([P, N_TILE, PACK], BF16, align_bytes=64, name="dy_grouped%d%d" % (n, h))
-                dy_codes = keep.tile([P, N_TILE], U32, align_bytes=64, name="dy_codes%d%d" % (n, h))
-                dy_scales = keep.tile([P, N_TILE], U8, align_bytes=64, name="dy_scales%d%d" % (n, h))
+                codes = keep.tile([P, N_TILE], U32, align_bytes=64, name="dy_codes%d%d" % (n, h))
+                scales = keep.tile([P, N_TILE], U8, align_bytes=64, name="dy_scales%d%d" % (n, h))
                 nc.vector.scalar_tensor_tensor(
                     out=dy_grouped[:],
                     in0=z_raw[n][:, :, px].rearrange("p j x -> p x j"),
@@ -115,26 +111,32 @@ def tile_prefusioncat_t_v_kernel(
                     op1=ALU.mult,
                 )
                 nc.vector.quantize_mx(
-                    out=dy_codes[:].bitcast(E5M2_X4),
-                    scales=dy_scales[:],
+                    out=codes[:].bitcast(E5M2_X4),
+                    scales=scales[:],
                     in_=dy_grouped[:].rearrange("p x j -> p (x j)"),
                 )
-                for t in range(M_TILES):
-                    acc = psum.tile([P, N_TILE], F32)
-                    nc.tensor.matmul_mx(
-                        out=acc[:],
-                        lhsT=w_codes[:, t * P : (t + 1) * P].bitcast(E4M3_X4),
-                        lhsT_scale=w_scales[:, t * P : (t + 1) * P],
-                        rhs=dy_codes[:].bitcast(E5M2_X4),
-                        rhs_scale=dy_scales[:],
-                        start=True,
-                        stop=True,
-                    )
-                    if banks_emptied % 3 == 2:
-                        nc.vector.tensor_copy(out=out_sb[:, t, px], in_=acc[:])
-                    else:
-                        nc.scalar.copy(out=out_sb[:, t, px], in_=acc[:])
-                    banks_emptied += 1
-                    if h == HALVES - 1 and t % STORE_TILES == STORE_TILES - 1:
-                        tiles = slice(t + 1 - STORE_TILES, t + 1)
-                        nc.sync.dma_start(out=out_by_tile[n, :, tiles, :], in_=out_sb[:, tiles, :])
+                dy_codes.append(codes)
+                dy_scales.append(scales)
+
+        out_by_pair = out.rearrange("n (a m b) h w -> n a m b (h w)", m=P, b=PAIR)
+        for n in range(IMAGES):
+            for a in range(PAIRS):
+                out_sb = keep.tile([P, PAIR, PIXELS], F32, name="out_sb%d%d" % (n, a))
+                for h in range(HALVES):
+                    px = slice(h * N_TILE, (h + 1) * N_TILE)
+                    for b in range(PAIR):
+                        acc = psum.tile([P, N_TILE], F32)
+                        nc.tensor.matmul_mx(
+                            out=acc[:],
+                            lhsT=w_codes[:, a, b, :].bitcast(E4M3_X4),
+                            lhsT_scale=w_scales[:, a, b, :],
+                            rhs=dy_codes[n * HALVES + h][:].bitcast(E5M2_X4),
+                            rhs_scale=dy_scales[n * HALVES + h][:],
+                            start=True,
+                            stop=True,
+                        )
+                        if n == IMAGES - 1 and b == PAIR - 1:
+                            nc.vector.tensor_copy(out=out_sb[:, b, px], in_=acc[:])
+                        else:
+                            nc.scalar.copy(out=out_sb[:, b, px], in_=acc[:])
+                nc.sync.dma_start(out=out_by_pair[n, a], in_=out_sb[:])

@@ -120,23 +120,30 @@ def tile_prefusioncat_t_v_kernel(
 
         out_by_pair = out.rearrange("n (a m b) h w -> n a m b (h w)", m=P, b=PAIR)
         for n in range(IMAGES):
-            for a in range(PAIRS):
-                out_sb = keep.tile([P, PAIR, PIXELS], F32, name="out_sb%d%d" % (n, a))
-                for h in range(HALVES):
-                    px = slice(h * N_TILE, (h + 1) * N_TILE)
-                    for b in range(PAIR):
-                        acc = psum.tile([P, N_TILE], F32)
-                        nc.tensor.matmul_mx(
-                            out=acc[:],
-                            lhsT=w_codes[:, a, b, :].bitcast(E4M3_X4),
-                            lhsT_scale=w_scales[:, a, b, :],
-                            rhs=dy_codes[n * HALVES + h][:].bitcast(E5M2_X4),
-                            rhs_scale=dy_scales[n * HALVES + h][:],
-                            start=True,
-                            stop=True,
-                        )
-                        if n == IMAGES - 1 and b == PAIR - 1:
-                            nc.vector.tensor_copy(out=out_sb[:, b, px], in_=acc[:])
-                        else:
-                            nc.scalar.copy(out=out_sb[:, b, px], in_=acc[:])
-                nc.sync.dma_start(out=out_by_pair[n, a], in_=out_sb[:])
+            halves_in_store = HALVES if n == IMAGES - 1 else 1
+            for first_half in range(0, HALVES, halves_in_store):
+                for a in range(PAIRS):
+                    out_sb = keep.tile(
+                        [P, PAIR, halves_in_store, N_TILE], F32, name="out_sb%d%d%d" % (n, first_half, a)
+                    )
+                    for i in range(halves_in_store):
+                        chunk = n * HALVES + first_half + i
+                        for b in range(PAIR):
+                            acc = psum.tile([P, N_TILE], F32)
+                            nc.tensor.matmul_mx(
+                                out=acc[:],
+                                lhsT=w_codes[:, a, b, :].bitcast(E4M3_X4),
+                                lhsT_scale=w_scales[:, a, b, :],
+                                rhs=dy_codes[chunk][:].bitcast(E5M2_X4),
+                                rhs_scale=dy_scales[chunk][:],
+                                start=True,
+                                stop=True,
+                            )
+                            if n == IMAGES - 1 and b == PAIR - 1:
+                                nc.vector.tensor_copy(out=out_sb[:, b, i, :], in_=acc[:])
+                            else:
+                                nc.scalar.copy(out=out_sb[:, b, i, :], in_=acc[:])
+                    px = slice(first_half * N_TILE, (first_half + halves_in_store) * N_TILE)
+                    nc.sync.dma_start(
+                        out=out_by_pair[n, a, :, :, px], in_=out_sb[:].rearrange("m b i x -> m b (i x)")
+                    )

@@ -43,6 +43,7 @@ def tile_prefusioncat_t_v_kernel(
     with ExitStack() as ctx:
         keep = ctx.enter_context(tc.tile_pool(name="keep", bufs=1))
         psum = ctx.enter_context(tc.psum_pool(name="psum", bufs=PSUM_BANKS))
+        ctx.enter_context(tc.manual_schedule())
 
         gamma_bf = keep.tile([P, PACK], BF16)
         var_bf = keep.tile([P, PACK], BF16)
@@ -81,42 +82,57 @@ def tile_prefusioncat_t_v_kernel(
         w_scales = keep.tile([P, PAIRS, PAIR, P], U8, align_bytes=64)
         w_by_pair = w_raw[:].rearrange("p j (a m b) -> p a b m j", m=P, b=PAIR)
         for a in range(PAIRS):
-            nc.vector.tensor_copy(out=w_grouped[:, a], in_=w_by_pair[:, a])
-        for a in range(0, PAIRS, 2):
+            if a < PAIRS // 2:
+                nc.vector.tensor_copy(out=w_grouped[:, a], in_=w_by_pair[:, a])
+            else:
+                nc.scalar.copy(out=w_grouped[:, a], in_=w_by_pair[:, a])
+
+        def quantise_w(a):
             nc.vector.quantize_mx(
                 out=w_codes[:, a : a + 2].rearrange("p a b m -> p (a b m)").bitcast(E4M3_X4),
                 scales=w_scales[:, a : a + 2].rearrange("p a b m -> p (a b m)"),
                 in_=w_grouped[:, a : a + 2].rearrange("p a b m j -> p (a b m j)"),
             )
 
-        dy_codes = []
-        dy_scales = []
-        for n in range(IMAGES):
-            g_scaled = keep.tile([P, PACK, PIXELS], BF16, name="g_scaled%d" % n)
+        g_scaled = [keep.tile([P, PACK, PIXELS], BF16, name="g_scaled%d" % n) for n in range(IMAGES)]
+        chunks = range(IMAGES * HALVES)
+        dy_grouped = [keep.tile([P, N_TILE, PACK], BF16, align_bytes=64, name="dy_grouped%d" % c) for c in chunks]
+        dy_codes = [keep.tile([P, N_TILE], U32, align_bytes=64, name="dy_codes%d" % c) for c in chunks]
+        dy_scales = [keep.tile([P, N_TILE], U8, align_bytes=64, name="dy_scales%d" % c) for c in chunks]
+
+        def scale_gradient(n):
             for j in range(PACK):
                 nc.vector.tensor_scalar_mul(
-                    out=g_scaled[:, j, :], in0=g_raw[n][:, j, :], scalar1=scale[:, j : j + 1]
+                    out=g_scaled[n][:, j, :], in0=g_raw[n][:, j, :], scalar1=scale[:, j : j + 1]
                 )
-            for h in range(HALVES):
-                px = slice(h * N_TILE, (h + 1) * N_TILE)
-                dy_grouped = keep.tile([P, N_TILE, PACK], BF16, align_bytes=64, name="dy_grouped%d%d" % (n, h))
-                codes = keep.tile([P, N_TILE], U32, align_bytes=64, name="dy_codes%d%d" % (n, h))
-                scales = keep.tile([P, N_TILE], U8, align_bytes=64, name="dy_scales%d%d" % (n, h))
-                nc.vector.scalar_tensor_tensor(
-                    out=dy_grouped[:],
-                    in0=z_raw[n][:, :, px].rearrange("p j x -> p x j"),
-                    scalar=0.0,
-                    in1=g_scaled[:, :, px].rearrange("p j x -> p x j"),
-                    op0=ALU.is_gt,
-                    op1=ALU.mult,
-                )
-                nc.vector.quantize_mx(
-                    out=codes[:].bitcast(E5M2_X4),
-                    scales=scales[:],
-                    in_=dy_grouped[:].rearrange("p x j -> p (x j)"),
-                )
-                dy_codes.append(codes)
-                dy_scales.append(scales)
+
+        def mask(c):
+            n, h = divmod(c, HALVES)
+            px = slice(h * N_TILE, (h + 1) * N_TILE)
+            nc.vector.scalar_tensor_tensor(
+                out=dy_grouped[c][:],
+                in0=z_raw[n][:, :, px].rearrange("p j x -> p x j"),
+                scalar=0.0,
+                in1=g_scaled[n][:, :, px].rearrange("p j x -> p x j"),
+                op0=ALU.is_gt,
+                op1=ALU.mult,
+            )
+
+        def quantise_dy(c):
+            nc.vector.quantize_mx(
+                out=dy_codes[c][:].bitcast(E5M2_X4),
+                scales=dy_scales[c][:],
+                in_=dy_grouped[c][:].rearrange("p x j -> p (x j)"),
+            )
+
+        quantise_w(0)
+        scale_gradient(0)
+        quantise_w(PAIRS // 2)
+        for c in chunks:
+            mask(c)
+            if c % HALVES == HALVES - 1 and c + 1 < len(chunks):
+                scale_gradient((c + 1) // HALVES)
+            quantise_dy(c)
 
         out_by_pair = out.rearrange("n (a m b) h w -> n a m b (h w)", m=P, b=PAIR)
         for n in range(IMAGES):

@@ -135,31 +135,24 @@ def tile_prefusioncat_t_v_kernel(
             quantise_dy(c)
 
         out_by_pair = out.rearrange("n (a m b) h w -> n a m b (h w)", m=P, b=PAIR)
-        for n in range(IMAGES):
-            halves_in_store = HALVES if n == IMAGES - 1 else 1
-            for first_half in range(0, HALVES, halves_in_store):
-                for a in range(PAIRS):
-                    out_sb = keep.tile(
-                        [P, PAIR, halves_in_store, N_TILE], F32, name="out_sb%d%d%d" % (n, first_half, a)
+        for c in chunks:
+            n, h = divmod(c, HALVES)
+            px = slice(h * N_TILE, (h + 1) * N_TILE)
+            for a in range(PAIRS):
+                out_sb = keep.tile([P, PAIR, N_TILE], F32, name="out_sb%d%d" % (c, a))
+                for b in range(PAIR):
+                    acc = psum.tile([P, N_TILE], F32)
+                    nc.tensor.matmul_mx(
+                        out=acc[:],
+                        lhsT=w_codes[:, a, b, :].bitcast(E4M3_X4),
+                        lhsT_scale=w_scales[:, a, b, :],
+                        rhs=dy_codes[c][:].bitcast(E5M2_X4),
+                        rhs_scale=dy_scales[c][:],
+                        start=True,
+                        stop=True,
                     )
-                    for i in range(halves_in_store):
-                        chunk = n * HALVES + first_half + i
-                        for b in range(PAIR):
-                            acc = psum.tile([P, N_TILE], F32)
-                            nc.tensor.matmul_mx(
-                                out=acc[:],
-                                lhsT=w_codes[:, a, b, :].bitcast(E4M3_X4),
-                                lhsT_scale=w_scales[:, a, b, :],
-                                rhs=dy_codes[chunk][:].bitcast(E5M2_X4),
-                                rhs_scale=dy_scales[chunk][:],
-                                start=True,
-                                stop=True,
-                            )
-                            if n == IMAGES - 1 and b == PAIR - 1:
-                                nc.vector.tensor_copy(out=out_sb[:, b, i, :], in_=acc[:])
-                            else:
-                                nc.scalar.copy(out=out_sb[:, b, i, :], in_=acc[:])
-                    px = slice(first_half * N_TILE, (first_half + halves_in_store) * N_TILE)
-                    nc.sync.dma_start(
-                        out=out_by_pair[n, a, :, :, px], in_=out_sb[:].rearrange("m b i x -> m b (i x)")
-                    )
+                    if c == len(chunks) - 1 and b == PAIR - 1:
+                        nc.vector.tensor_copy(out=out_sb[:, b, :], in_=acc[:])
+                    else:
+                        nc.scalar.copy(out=out_sb[:, b, :], in_=acc[:])
+                nc.sync.dma_start(out=out_by_pair[n, a, :, :, px], in_=out_sb[:])

@@ -62,9 +62,12 @@ def tile_prefusioncat_t_v_kernel(
                 in_=grad_out[n, OUT_CH : 2 * OUT_CH].rearrange("(p j) h w -> p j (h w)", j=PACK),
             )
             z_dram = pts_z[n].rearrange("(p j) h w -> p j (h w)", j=PACK)
-            for h in range(HALVES):
-                px = slice(h * N_TILE, (h + 1) * N_TILE)
-                nc.sync.dma_start(out=z_n[:, :, px], in_=z_dram[:, :, px])
+            if n == 0:
+                for h in range(HALVES):
+                    px = slice(h * N_TILE, (h + 1) * N_TILE)
+                    nc.sync.dma_start(out=z_n[:, :, px], in_=z_dram[:, :, px])
+            else:
+                nc.sync.dma_start(out=z_n[:], in_=z_dram)
             g_raw.append(g_n)
             z_raw.append(z_n)
 

@@ -51,7 +51,6 @@ def tile_prefusioncat_t_v_kernel(
         nc.scalar.dma_start(out=gamma_bf[:], in_=pts_gamma.rearrange("(p j) -> p j", j=PACK))
 
         w_raw = keep.tile([P, PACK, IN_CH], BF16)
-        nc.sync.dma_start(out=w_raw[:], in_=pts_w.rearrange("(p j) c -> p j c", j=PACK))
         g_raw = []
         z_raw = []
         for n in range(IMAGES):
@@ -66,6 +65,8 @@ def tile_prefusioncat_t_v_kernel(
                 for h in range(HALVES):
                     px = slice(h * N_TILE, (h + 1) * N_TILE)
                     nc.sync.dma_start(out=z_n[:, :, px], in_=z_dram[:, :, px])
+                    if h == 0:
+                        nc.sync.dma_start(out=w_raw[:], in_=pts_w.rearrange("(p j) c -> p j c", j=PACK))
             else:
                 nc.sync.dma_start(out=z_n[:], in_=z_dram)
             g_raw.append(g_n)
@@ -84,11 +85,12 @@ def tile_prefusioncat_t_v_kernel(
         w_codes = keep.tile([P, PAIRS, PAIR, P], U32, align_bytes=64)
         w_scales = keep.tile([P, PAIRS, PAIR, P], U8, align_bytes=64)
         w_by_pair = w_raw[:].rearrange("p j (a m b) -> p a b m j", m=P, b=PAIR)
-        for a in range(PAIRS):
-            if a < PAIRS // 2:
-                nc.vector.tensor_copy(out=w_grouped[:, a], in_=w_by_pair[:, a])
-            else:
-                nc.scalar.copy(out=w_grouped[:, a], in_=w_by_pair[:, a])
+        def regroup_w():
+            for a in range(PAIRS):
+                if a < PAIRS // 2:
+                    nc.vector.tensor_copy(out=w_grouped[:, a], in_=w_by_pair[:, a])
+                else:
+                    nc.scalar.copy(out=w_grouped[:, a], in_=w_by_pair[:, a])
 
         def quantise_w(a):
             nc.vector.quantize_mx(
@@ -128,14 +130,19 @@ def tile_prefusioncat_t_v_kernel(
                 in_=dy_grouped[c][:].rearrange("p x j -> p (x j)"),
             )
 
-        quantise_w(0)
         scale_gradient(0)
+        mask(0)
+        regroup_w()
+        quantise_dy(0)
+        quantise_w(0)
+        mask(1)
         quantise_w(PAIRS // 2)
-        for c in chunks:
-            mask(c)
-            if c % HALVES == HALVES - 1 and c + 1 < len(chunks):
-                scale_gradient((c + 1) // HALVES)
-            quantise_dy(c)
+        quantise_dy(1)
+        scale_gradient(1)
+        mask(2)
+        quantise_dy(2)
+        mask(3)
+        quantise_dy(3)
 
         out_by_pair = out.rearrange("n (a m b) h w -> n a m b (h w)", m=P, b=PAIR)
         for c in chunks:

@@ -135,8 +135,8 @@ def tile_prefusioncat_t_v_kernel(
         regroup_w()
         quantise_dy(0)
         quantise_w(0)
-        mask(1)
         quantise_w(PAIRS // 2)
+        mask(1)
         quantise_dy(1)
         scale_gradient(1)
         mask(2)
@@ -145,24 +145,35 @@ def tile_prefusioncat_t_v_kernel(
         quantise_dy(3)
 
         out_by_pair = out.rearrange("n (a m b) h w -> n a m b (h w)", m=P, b=PAIR)
-        for c in chunks:
+        last = IMAGES - 1
+        steps = [(c, a) for c in chunks for a in range(PAIRS) if (c // HALVES, a) != (last, PAIRS - 1)]
+        steps += [(last * HALVES + h, PAIRS - 1) for h in range(HALVES)]
+        whole_sb = keep.tile([P, PAIR, HALVES, N_TILE], F32)
+        for c, a in steps:
             n, h = divmod(c, HALVES)
             px = slice(h * N_TILE, (h + 1) * N_TILE)
-            for a in range(PAIRS):
-                out_sb = keep.tile([P, PAIR, N_TILE], F32, name="out_sb%d%d" % (c, a))
-                for b in range(PAIR):
-                    acc = psum.tile([P, N_TILE], F32)
-                    nc.tensor.matmul_mx(
-                        out=acc[:],
-                        lhsT=w_codes[:, a, b, :].bitcast(E4M3_X4),
-                        lhsT_scale=w_scales[:, a, b, :],
-                        rhs=dy_codes[c][:].bitcast(E5M2_X4),
-                        rhs_scale=dy_scales[c][:],
-                        start=True,
-                        stop=True,
-                    )
-                    if c == len(chunks) - 1 and b == PAIR - 1:
-                        nc.vector.tensor_copy(out=out_sb[:, b, :], in_=acc[:])
-                    else:
-                        nc.scalar.copy(out=out_sb[:, b, :], in_=acc[:])
-                nc.sync.dma_start(out=out_by_pair[n, a, :, :, px], in_=out_sb[:])
+            whole = (n, a) == (last, PAIRS - 1)
+            if whole:
+                out_sb = whole_sb[:, :, h, :]
+            else:
+                half_sb = keep.tile([P, PAIR, N_TILE], F32, name="half_sb%d%d" % (c, a))
+                out_sb = half_sb[:]
+            for b in range(PAIR):
+                acc = psum.tile([P, N_TILE], F32)
+                nc.tensor.matmul_mx(
+                    out=acc[:],
+                    lhsT=w_codes[:, a, b, :].bitcast(E4M3_X4),
+                    lhsT_scale=w_scales[:, a, b, :],
+                    rhs=dy_codes[c][:].bitcast(E5M2_X4),
+                    rhs_scale=dy_scales[c][:],
+                    start=True,
+                    stop=True,
+                )
+                if b == PAIR - 1 and (c == len(chunks) - 1 or whole):
+                    nc.vector.tensor_copy(out=out_sb[:, b, :], in_=acc[:])
+                else:
+                    nc.scalar.copy(out=out_sb[:, b, :], in_=acc[:])
+            if not whole:
+                nc.sync.dma_start(out=out_by_pair[n, a, :, :, px], in_=out_sb)
+            elif h == HALVES - 1:
+                nc.sync.dma_start(out=out_by_pair[n, a], in_=whole_sb[:].rearrange("m b i x -> m b (i x)"))

@@ -21,6 +21,7 @@ HALVES = PIXELS // N_TILE
 PAIR = 2
 PAIRS = IN_CH // (P * PAIR)
 PSUM_BANKS = 8
+WHOLE_PAIRS = 2
 BN_EPS = 1e-5
 
 FLOPS = 2 * IMAGES * PIXELS * IN_CH * OUT_CH
@@ -87,7 +88,7 @@ def tile_prefusioncat_t_v_kernel(
         w_by_pair = w_raw[:].rearrange("p j (a m b) -> p a b m j", m=P, b=PAIR)
         def regroup_w():
             for a in range(PAIRS):
-                if a < PAIRS // 2:
+                if a == 0:
                     nc.vector.tensor_copy(out=w_grouped[:, a], in_=w_by_pair[:, a])
                 else:
                     nc.scalar.copy(out=w_grouped[:, a], in_=w_by_pair[:, a])
@@ -135,8 +136,8 @@ def tile_prefusioncat_t_v_kernel(
         regroup_w()
         quantise_dy(0)
         quantise_w(0)
-        quantise_w(PAIRS // 2)
         mask(1)
+        quantise_w(PAIRS // 2)
         quantise_dy(1)
         scale_gradient(1)
         mask(2)
@@ -146,14 +147,16 @@ def tile_prefusioncat_t_v_kernel(
 
         out_by_pair = out.rearrange("n (a m b) h w -> n a m b (h w)", m=P, b=PAIR)
         last = IMAGES - 1
-        steps = [(c, a) for c in chunks for a in range(PAIRS) if (c // HALVES, a) != (last, PAIRS - 1)]
-        steps += [(last * HALVES + h, PAIRS - 1) for h in range(HALVES)]
-        whole_sb = keep.tile([P, PAIR, HALVES, N_TILE], F32)
+        whole_pairs = range(PAIRS - WHOLE_PAIRS, PAIRS)
+        steps = [(c, a) for c in chunks for a in range(PAIRS) if not (c // HALVES == last and a in whole_pairs)]
+        steps += [(last * HALVES + h, a) for a in whole_pairs for h in range(HALVES)]
+        whole_sbs = [keep.tile([P, PAIR, HALVES, N_TILE], F32, name="whole_sb%d" % a) for a in whole_pairs]
         for c, a in steps:
             n, h = divmod(c, HALVES)
             px = slice(h * N_TILE, (h + 1) * N_TILE)
-            whole = (n, a) == (last, PAIRS - 1)
+            whole = n == last and a in whole_pairs
             if whole:
+                whole_sb = whole_sbs[a - whole_pairs[0]]
                 out_sb = whole_sb[:, :, h, :]
             else:
                 half_sb = keep.tile([P, PAIR, N_TILE], F32, name="half_sb%d%d" % (c, a))

@@ -20,7 +20,8 @@ N_TILE = 512
 HALVES = PIXELS // N_TILE
 PAIR = 2
 PAIRS = IN_CH // (P * PAIR)
-PSUM_BANKS = 8
+SCALAR_BANKS = 5
+VECTOR_BANKS = 3
 WHOLE_PAIRS = 2
 BN_EPS = 1e-5
 
@@ -43,7 +44,8 @@ def tile_prefusioncat_t_v_kernel(
     nc = tc.nc
     with ExitStack() as ctx:
         keep = ctx.enter_context(tc.tile_pool(name="keep", bufs=1))
-        psum = ctx.enter_context(tc.psum_pool(name="psum", bufs=PSUM_BANKS))
+        scalar_psum = ctx.enter_context(tc.psum_pool(name="scalar_psum", bufs=SCALAR_BANKS))
+        vector_psum = ctx.enter_context(tc.psum_pool(name="vector_psum", bufs=VECTOR_BANKS))
         ctx.enter_context(tc.manual_schedule())
 
         gamma_bf = keep.tile([P, PACK], BF16)
@@ -148,35 +150,39 @@ def tile_prefusioncat_t_v_kernel(
         out_by_pair = out.rearrange("n (a m b) h w -> n a m b (h w)", m=P, b=PAIR)
         last = IMAGES - 1
         whole_pairs = range(PAIRS - WHOLE_PAIRS, PAIRS)
-        steps = [(c, a) for c in chunks for a in range(PAIRS) if not (c // HALVES == last and a in whole_pairs)]
-        steps += [(last * HALVES + h, a) for a in whole_pairs for h in range(HALVES)]
         whole_sbs = [keep.tile([P, PAIR, HALVES, N_TILE], F32, name="whole_sb%d" % a) for a in whole_pairs]
-        for c, a in steps:
+        vector_pairs = (0, 1, 3)
+        for c in chunks:
             n, h = divmod(c, HALVES)
             px = slice(h * N_TILE, (h + 1) * N_TILE)
-            whole = n == last and a in whole_pairs
-            if whole:
-                whole_sb = whole_sbs[a - whole_pairs[0]]
-                out_sb = whole_sb[:, :, h, :]
-            else:
-                half_sb = keep.tile([P, PAIR, N_TILE], F32, name="half_sb%d%d" % (c, a))
-                out_sb = half_sb[:]
-            for b in range(PAIR):
-                acc = psum.tile([P, N_TILE], F32)
-                nc.tensor.matmul_mx(
-                    out=acc[:],
-                    lhsT=w_codes[:, a, b, :].bitcast(E4M3_X4),
-                    lhsT_scale=w_scales[:, a, b, :],
-                    rhs=dy_codes[c][:].bitcast(E5M2_X4),
-                    rhs_scale=dy_scales[c][:],
-                    start=True,
-                    stop=True,
-                )
-                if b == PAIR - 1 and (c == len(chunks) - 1 or whole):
-                    nc.vector.tensor_copy(out=out_sb[:, b, :], in_=acc[:])
+            for a in range(PAIRS):
+                whole = n == last and a in whole_pairs
+                if whole:
+                    whole_sb = whole_sbs[a - whole_pairs[0]]
+                    out_sb = whole_sb[:, :, h, :]
                 else:
-                    nc.scalar.copy(out=out_sb[:, b, :], in_=acc[:])
-            if not whole:
-                nc.sync.dma_start(out=out_by_pair[n, a, :, :, px], in_=out_sb)
-            elif h == HALVES - 1:
-                nc.sync.dma_start(out=out_by_pair[n, a], in_=whole_sb[:].rearrange("m b i x -> m b (i x)"))
+                    half_sb = keep.tile([P, PAIR, N_TILE], F32, name="half_sb%d%d" % (c, a))
+                    out_sb = half_sb[:]
+                by_vector = c == len(chunks) - 1 and a in vector_pairs
+                for b in range(PAIR):
+                    if by_vector:
+                        acc = vector_psum.tile([P, N_TILE], F32, name="vector_acc")
+                    else:
+                        acc = scalar_psum.tile([P, N_TILE], F32, name="scalar_acc")
+                    nc.tensor.matmul_mx(
+                        out=acc[:],
+                        lhsT=w_codes[:, a, b, :].bitcast(E4M3_X4),
+                        lhsT_scale=w_scales[:, a, b, :],
+                        rhs=dy_codes[c][:].bitcast(E5M2_X4),
+                        rhs_scale=dy_scales[c][:],
+                        start=True,
+                        stop=True,
+                    )
+                    if by_vector:
+                        nc.vector.tensor_copy(out=out_sb[:, b, :], in_=acc[:])
+                    else:
+                        nc.scalar.copy(out=out_sb[:, b, :], in_=acc[:])
+                if not whole:
+                    nc.sync.dma_start(out=out_by_pair[n, a, :, :, px], in_=out_sb)
+                elif h == HALVES - 1:
+                    nc.sync.dma_start(out=out_by_pair[n, a], in_=whole_sb[:].rearrange("m b i x -> m b (i x)"))

@@ -20,9 +20,9 @@ N_TILE = 512
 HALVES = PIXELS // N_TILE
 PAIR = 2
 PAIRS = IN_CH // (P * PAIR)
-SCALAR_BANKS = 5
-VECTOR_BANKS = 3
-WHOLE_PAIRS = 2
+SCALAR_BANKS = 4
+VECTOR_BANKS = 4
+WHOLE = ((0, 3), (1, 2), (1, 3))
 BN_EPS = 1e-5
 
 FLOPS = 2 * IMAGES * PIXELS * IN_CH * OUT_CH
@@ -133,6 +133,38 @@ def tile_prefusioncat_t_v_kernel(
                 in_=dy_grouped[c][:].rearrange("p x j -> p (x j)"),
             )
 
+        out_by_pair = out.rearrange("n (a m b) h w -> n a m b (h w)", m=P, b=PAIR)
+        out_sb = [
+            [keep.tile([P, PAIR, HALVES, N_TILE], F32, name="out_sb%d%d" % (n, a)) for a in range(PAIRS)]
+            for n in range(IMAGES)
+        ]
+
+        def passes(c, a, by_vector=()):
+            n, h = divmod(c, HALVES)
+            for b in range(PAIR):
+                if b in by_vector:
+                    acc = vector_psum.tile([P, N_TILE], F32, name="vector_acc")
+                else:
+                    acc = scalar_psum.tile([P, N_TILE], F32, name="scalar_acc")
+                nc.tensor.matmul_mx(
+                    out=acc[:],
+                    lhsT=w_codes[:, a, b, :].bitcast(E4M3_X4),
+                    lhsT_scale=w_scales[:, a, b, :],
+                    rhs=dy_codes[c][:].bitcast(E5M2_X4),
+                    rhs_scale=dy_scales[c][:],
+                    start=True,
+                    stop=True,
+                )
+                if b in by_vector:
+                    nc.vector.tensor_copy(out=out_sb[n][a][:, b, h, :], in_=acc[:])
+                else:
+                    nc.scalar.copy(out=out_sb[n][a][:, b, h, :], in_=acc[:])
+            if (n, a) not in WHOLE:
+                px = slice(h * N_TILE, (h + 1) * N_TILE)
+                nc.sync.dma_start(out=out_by_pair[n, a, :, :, px], in_=out_sb[n][a][:, :, h, :])
+            elif h == HALVES - 1:
+                nc.sync.dma_start(out=out_by_pair[n, a], in_=out_sb[n][a][:].rearrange("m b i x -> m b (i x)"))
+
         scale_gradient(0)
         mask(0)
         regroup_w()
@@ -142,47 +174,21 @@ def tile_prefusioncat_t_v_kernel(
         quantise_w(PAIRS // 2)
         quantise_dy(1)
         scale_gradient(1)
+        for a in range(3):
+            passes(0, a)
+        passes(1, 0, by_vector=(0, 1))
+        passes(1, 1)
+        passes(1, 2)
+        passes(0, 3)
+        passes(1, 3)
         mask(2)
         quantise_dy(2)
+        for a in range(3):
+            passes(2, a)
         mask(3)
         quantise_dy(3)
-
-        out_by_pair = out.rearrange("n (a m b) h w -> n a m b (h w)", m=P, b=PAIR)
-        last = IMAGES - 1
-        whole_pairs = range(PAIRS - WHOLE_PAIRS, PAIRS)
-        whole_sbs = [keep.tile([P, PAIR, HALVES, N_TILE], F32, name="whole_sb%d" % a) for a in whole_pairs]
-        vector_pairs = (0, 1, 3)
-        for c in chunks:
-            n, h = divmod(c, HALVES)
-            px = slice(h * N_TILE, (h + 1) * N_TILE)
-            for a in range(PAIRS):
-                whole = n == last and a in whole_pairs
-                if whole:
-                    whole_sb = whole_sbs[a - whole_pairs[0]]
-                    out_sb = whole_sb[:, :, h, :]
-                else:
-                    half_sb = keep.tile([P, PAIR, N_TILE], F32, name="half_sb%d%d" % (c, a))
-                    out_sb = half_sb[:]
-                by_vector = c == len(chunks) - 1 and a in vector_pairs
-                for b in range(PAIR):
-                    if by_vector:
-                        acc = vector_psum.tile([P, N_TILE], F32, name="vector_acc")
-                    else:
-                        acc = scalar_psum.tile([P, N_TILE], F32, name="scalar_acc")
-                    nc.tensor.matmul_mx(
-                        out=acc[:],
-                        lhsT=w_codes[:, a, b, :].bitcast(E4M3_X4),
-                        lhsT_scale=w_scales[:, a, b, :],
-                        rhs=dy_codes[c][:].bitcast(E5M2_X4),
-                        rhs_scale=dy_scales[c][:],
-                        start=True,
-                        stop=True,
-                    )
-                    if by_vector:
-                        nc.vector.tensor_copy(out=out_sb[:, b, :], in_=acc[:])
-                    else:
-                        nc.scalar.copy(out=out_sb[:, b, :], in_=acc[:])
-                if not whole:
-                    nc.sync.dma_start(out=out_by_pair[n, a, :, :, px], in_=out_sb)
-                elif h == HALVES - 1:
-                    nc.sync.dma_start(out=out_by_pair[n, a], in_=whole_sb[:].rearrange("m b i x -> m b (i x)"))
+        passes(3, 0, by_vector=(0,))
+        passes(3, 1, by_vector=(0,))
+        passes(2, 3)
+        passes(3, 2, by_vector=(0, 1))
+        passes(3, 3, by_vector=(0, 1))

from contextlib import ExitStack

import concourse.mybir as mybir

BF16 = mybir.dt.bfloat16
F32 = mybir.dt.float32
U32 = mybir.dt.uint32
U8 = mybir.dt.uint8
E4M3_X4 = mybir.dt.float8_e4m3fn_x4
E5M2_X4 = mybir.dt.float8_e5m2_x4
ALU = mybir.AluOpType

P = 128
PACK = 4
IMAGES = 2
OUT_CH = 512
IN_CH = 1024
PIXELS = 1024
N_TILE = 512
HALVES = PIXELS // N_TILE
PAIR = 2
PAIRS = IN_CH // (P * PAIR)
SCALAR_BANKS = 4
VECTOR_BANKS = 4
WHOLE = ((0, 3), (1, 2), (1, 3))
BN_EPS = 1e-5

FLOPS = 2 * IMAGES * PIXELS * IN_CH * OUT_CH
BYTES = (
    IMAGES * OUT_CH * PIXELS * (2 + 4)
    + OUT_CH * IN_CH * 2
    + 2 * OUT_CH * 2
    + IMAGES * IN_CH * PIXELS * 4
)


def tile_prefusioncat_t_v_kernel(
    tc,
    img_feat0, img_feat1, img_feat2, img_feat3, img_feat4, pts_feat0,
    img_w, img_b, img_gamma, img_beta, img_mean, img_var,
    pts_w, pts_b, pts_gamma, pts_beta, pts_mean, pts_var, pts_z, grad_out,
    out,
):
    nc = tc.nc
    with ExitStack() as ctx:
        keep = ctx.enter_context(tc.tile_pool(name="keep", bufs=1))
        scalar_psum = ctx.enter_context(tc.psum_pool(name="scalar_psum", bufs=SCALAR_BANKS))
        vector_psum = ctx.enter_context(tc.psum_pool(name="vector_psum", bufs=VECTOR_BANKS))
        ctx.enter_context(tc.manual_schedule())

        gamma_bf = keep.tile([P, PACK], BF16)
        var_bf = keep.tile([P, PACK], BF16)
        nc.scalar.dma_start(out=var_bf[:], in_=pts_var.rearrange("(p j) -> p j", j=PACK))
        nc.scalar.dma_start(out=gamma_bf[:], in_=pts_gamma.rearrange("(p j) -> p j", j=PACK))

        w_raw = keep.tile([P, PACK, IN_CH], BF16)
        g_raw = []
        z_raw = []
        for n in range(IMAGES):
            g_n = keep.tile([P, PACK, PIXELS], BF16, name="g_raw%d" % n)
            z_n = keep.tile([P, PACK, PIXELS], F32, name="z_raw%d" % n)
            nc.sync.dma_start(
                out=g_n[:],
                in_=grad_out[n, OUT_CH : 2 * OUT_CH].rearrange("(p j) h w -> p j (h w)", j=PACK),
            )
            z_dram = pts_z[n].rearrange("(p j) h w -> p j (h w)", j=PACK)
            if n == 0:
                for h in range(HALVES):
                    px = slice(h * N_TILE, (h + 1) * N_TILE)
                    nc.sync.dma_start(out=z_n[:, :, px], in_=z_dram[:, :, px])
                    if h == 0:
                        nc.sync.dma_start(out=w_raw[:], in_=pts_w.rearrange("(p j) c -> p j c", j=PACK))
            else:
                nc.sync.dma_start(out=z_n[:], in_=z_dram)
            g_raw.append(g_n)
            z_raw.append(z_n)

        var_eps = keep.tile([P, PACK], F32)
        std = keep.tile([P, PACK], F32)
        inv_std = keep.tile([P, PACK], F32)
        scale = keep.tile([P, PACK], F32)
        nc.vector.tensor_scalar_add(out=var_eps[:], in0=var_bf[:], scalar1=BN_EPS)
        nc.scalar.sqrt(std[:], var_eps[:])
        nc.vector.reciprocal(out=inv_std[:], in_=std[:])
        nc.vector.tensor_mul(out=scale[:], in0=inv_std[:], in1=gamma_bf[:])

        w_grouped = keep.tile([P, PAIRS, PAIR, P, PACK], BF16, align_bytes=64)
        w_codes = keep.tile([P, PAIRS, PAIR, P], U32, align_bytes=64)
        w_scales = keep.tile([P, PAIRS, PAIR, P], U8, align_bytes=64)
        w_by_pair = w_raw[:].rearrange("p j (a m b) -> p a b m j", m=P, b=PAIR)
        def regroup_w():
            for a in range(PAIRS):
                if a == 0:
                    nc.vector.tensor_copy(out=w_grouped[:, a], in_=w_by_pair[:, a])
                else:
                    nc.scalar.copy(out=w_grouped[:, a], in_=w_by_pair[:, a])

        def quantise_w(a):
            nc.vector.quantize_mx(
                out=w_codes[:, a : a + 2].rearrange("p a b m -> p (a b m)").bitcast(E4M3_X4),
                scales=w_scales[:, a : a + 2].rearrange("p a b m -> p (a b m)"),
                in_=w_grouped[:, a : a + 2].rearrange("p a b m j -> p (a b m j)"),
            )

        g_scaled = [keep.tile([P, PACK, PIXELS], BF16, name="g_scaled%d" % n) for n in range(IMAGES)]
        chunks = range(IMAGES * HALVES)
        dy_grouped = [keep.tile([P, N_TILE, PACK], BF16, align_bytes=64, name="dy_grouped%d" % c) for c in chunks]
        dy_codes = [keep.tile([P, N_TILE], U32, align_bytes=64, name="dy_codes%d" % c) for c in chunks]
        dy_scales = [keep.tile([P, N_TILE], U8, align_bytes=64, name="dy_scales%d" % c) for c in chunks]

        def scale_gradient(n):
            for j in range(PACK):
                nc.vector.tensor_scalar_mul(
                    out=g_scaled[n][:, j, :], in0=g_raw[n][:, j, :], scalar1=scale[:, j : j + 1]
                )

        def mask(c):
            n, h = divmod(c, HALVES)
            px = slice(h * N_TILE, (h + 1) * N_TILE)
            nc.vector.scalar_tensor_tensor(
                out=dy_grouped[c][:],
                in0=z_raw[n][:, :, px].rearrange("p j x -> p x j"),
                scalar=0.0,
                in1=g_scaled[n][:, :, px].rearrange("p j x -> p x j"),
                op0=ALU.is_gt,
                op1=ALU.mult,
            )

        def quantise_dy(c):
            nc.vector.quantize_mx(
                out=dy_codes[c][:].bitcast(E5M2_X4),
                scales=dy_scales[c][:],
                in_=dy_grouped[c][:].rearrange("p x j -> p (x j)"),
            )

        out_by_pair = out.rearrange("n (a m b) h w -> n a m b (h w)", m=P, b=PAIR)
        out_sb = [
            [keep.tile([P, PAIR, HALVES, N_TILE], F32, name="out_sb%d%d" % (n, a)) for a in range(PAIRS)]
            for n in range(IMAGES)
        ]

        def passes(c, a, by_vector=()):
            n, h = divmod(c, HALVES)
            for b in range(PAIR):
                if b in by_vector:
                    acc = vector_psum.tile([P, N_TILE], F32, name="vector_acc")
                else:
                    acc = scalar_psum.tile([P, N_TILE], F32, name="scalar_acc")
                nc.tensor.matmul_mx(
                    out=acc[:],
                    lhsT=w_codes[:, a, b, :].bitcast(E4M3_X4),
                    lhsT_scale=w_scales[:, a, b, :],
                    rhs=dy_codes[c][:].bitcast(E5M2_X4),
                    rhs_scale=dy_scales[c][:],
                    start=True,
                    stop=True,
                )
                if b in by_vector:
                    nc.vector.tensor_copy(out=out_sb[n][a][:, b, h, :], in_=acc[:])
                else:
                    nc.scalar.copy(out=out_sb[n][a][:, b, h, :], in_=acc[:])
            if (n, a) not in WHOLE:
                px = slice(h * N_TILE, (h + 1) * N_TILE)
                nc.sync.dma_start(out=out_by_pair[n, a, :, :, px], in_=out_sb[n][a][:, :, h, :])
            elif h == HALVES - 1:
                nc.sync.dma_start(out=out_by_pair[n, a], in_=out_sb[n][a][:].rearrange("m b i x -> m b (i x)"))

        scale_gradient(0)
        mask(0)
        regroup_w()
        quantise_dy(0)
        quantise_w(0)
        mask(1)
        quantise_w(PAIRS // 2)
        quantise_dy(1)
        scale_gradient(1)
        for a in range(3):
            passes(0, a)
        passes(1, 0, by_vector=(0, 1))
        passes(1, 1)
        passes(1, 2)
        passes(0, 3)
        passes(1, 3)
        mask(2)
        quantise_dy(2)
        for a in range(3):
            passes(2, a)
        mask(3)
        quantise_dy(3)
        passes(3, 0, by_vector=(0,))
        passes(3, 1, by_vector=(0,))
        passes(2, 3)
        passes(3, 2, by_vector=(0, 1))
        passes(3, 3, by_vector=(0, 1))
